import numpy as np
import ml_dtypes


def mxq(x, axis, fmt="e4m3"):
    dtype, down = {"e4m3": (ml_dtypes.float8_e4m3fn, 7), "e5m2": (ml_dtypes.float8_e5m2, 14)}[fmt]
    v = np.moveaxis(np.asarray(x, np.float32).astype(ml_dtypes.bfloat16).astype(np.float64), axis, -1)
    blocks = v.reshape(v.shape[:-1] + (-1, 32))
    amax = np.abs(blocks).max(-1, keepdims=True)
    byte = np.maximum(np.where(amax > 0, np.frexp(amax)[1] - 1 + 127, 0) - down, 1)
    scale = np.exp2(byte - 127.0)
    codes = (blocks / scale).astype(np.float32).astype(dtype).astype(np.float64)
    return np.moveaxis((codes * scale).reshape(v.shape), -1, axis)


WIDE = False


def mx_kscale(k):
    if not WIDE:
        return np.ones(k)
    levels = np.array([10, -10, 5, -5, 0])
    a = np.random.permutation(np.resize(levels, k // 512 * 4)).reshape(k // 512, 4)
    idx = np.arange(k)
    return np.exp2(a[idx // 512, idx % 128 // 32])


BF16 = ml_dtypes.bfloat16


def bf(x):
    return np.asarray(x, np.float32).astype(BF16)


def f64(x):
    return np.asarray(x).astype(np.float64)


E2M1 = np.array([0.0, 0.5, 1.0, 1.5, 2.0, 3.0, 4.0, 6.0, -0.0, -0.5, -1.0, -1.5, -2.0, -3.0, -4.0, -6.0])


def pack_weight(w, fmt):
    k, n = w.shape
    w = f64(bf(w)).reshape(k // 32, 32, n)
    amax = np.abs(w).max(1)
    if fmt == "e4m3":
        byte = np.frexp(amax)[1] - 1 + 127 - 7
    else:
        mant, ex = np.frexp(amax / 6.0)
        byte = np.where(mant > 0.5, ex, ex - 1) + 127
    byte = np.clip(np.where(amax > 0, byte, 1), 1, 254)
    scaled = (w * np.exp2(127.0 - byte)[:, None, :]).reshape(k, n).astype(np.float32)
    by_word = np.ascontiguousarray(scaled.reshape(k // 512, 128, 4, n).transpose(0, 1, 3, 2))
    if fmt == "e4m3":
        words = by_word.astype(ml_dtypes.float8_e4m3fn).view(np.uint8)
    else:
        c = by_word.astype(ml_dtypes.float4_e2m1fn).view(np.uint8) & 0xF
        words = c[..., 0::2] | (c[..., 1::2] << 4)
    return np.ascontiguousarray(words), np.ascontiguousarray(byte.astype(np.uint8).reshape(k // 512, 16, n))


def unpack_weight(words, scales, fmt):
    g, p, n, _ = words.shape
    if fmt == "e4m3":
        vals = np.ascontiguousarray(words).view(ml_dtypes.float8_e4m3fn).astype(np.float64)
    else:
        nib = np.empty((g, p, n, 4), np.uint8)
        nib[..., 0::2] = words & 0xF
        nib[..., 1::2] = words >> 4
        vals = E2M1[nib]
    vals = vals * np.repeat(np.exp2(scales.astype(np.float64) - 127.0), 8, axis=1)[..., None]
    return vals.transpose(0, 1, 3, 2).reshape(g * 512, n)


B, IN_F, OUT_F = 256, 4096, 4096
IN_Q = IN_F // 4
OUT_Q = OUT_F // 4
FMT = "e4m3"


def setup_inputs():
    s = mx_kscale(IN_Q)
    scale = 1.0 / np.sqrt(IN_Q)
    inp = {"x": bf((np.random.standard_normal((B, 4, IN_Q)) * s).reshape(B, IN_F))}
    for name in ["rr", "ri", "rj", "rk"]:
        w = np.random.uniform(-scale, scale, (OUT_Q, IN_Q)) / s[None, :]
        words, scales = pack_weight(np.ascontiguousarray(w.T), FMT)
        inp["W_" + name + "_words"] = words
        inp["W_" + name + "_scales"] = scales
    for name in ["rr", "ri", "rj", "rk"]:
        inp["b_" + name] = bf(np.random.standard_normal(OUT_Q) * 0.5)
    return inp


def reference(x, W_rr_words, W_rr_scales, W_ri_words, W_ri_scales, W_rj_words, W_rj_scales, W_rk_words, W_rk_scales, b_rr, b_ri, b_rj, b_rk):
    b = x.shape[0]
    xs = f64(x).reshape(b, 4, IN_Q)
    bias = np.stack([f64(b_rr), f64(b_ri), f64(b_rj), f64(b_rk)])
    xq = mxq(xs, 2, "e4m3")
    Wq = np.stack([
        unpack_weight(W_rr_words, W_rr_scales, FMT).T,
        unpack_weight(W_ri_words, W_ri_scales, FMT).T,
        unpack_weight(W_rj_words, W_rj_scales, FMT).T,
        unpack_weight(W_rk_words, W_rk_scales, FMT).T,
    ])
    Y = (xq.reshape(b * 4, IN_Q) @ Wq.reshape(4 * OUT_Q, IN_Q).T).reshape(b, 4, 4, OUT_Q) + bias
    out_r = Y[:, 0, 0] - Y[:, 1, 1] - Y[:, 2, 2] - Y[:, 3, 3]
    out_i = Y[:, 0, 1] + Y[:, 1, 0] + Y[:, 2, 3] - Y[:, 3, 2]
    out_j = Y[:, 0, 2] - Y[:, 1, 3] + Y[:, 2, 0] + Y[:, 3, 1]
    out_k = Y[:, 0, 3] + Y[:, 1, 2] - Y[:, 2, 1] + Y[:, 3, 0]
    out = np.stack([out_r, out_i, out_j, out_k], axis=1)
    return out.reshape(b, -1)

@@ -1,0 +1,200 @@
+from contextlib import ExitStack
+
+import concourse.mybir as mybir
+from concourse.masks import make_identity
+
+F32 = mybir.dt.float32
+BF16 = mybir.dt.bfloat16
+I32 = mybir.dt.int32
+U32 = mybir.dt.uint32
+U8 = mybir.dt.uint8
+FP8X4 = mybir.dt.float8_e4m3fn_x4
+ALU = mybir.AluOpType
+
+P = 128
+PACK = 4
+K_PASS = P * PACK
+ROWS = 256
+CHUNK = 1024
+PARTS = 4
+PASSES = CHUNK // K_PASS
+ROW_BLOCKS = ROWS // P
+N_TILE = 512
+COL_HALVES = CHUNK // N_TILE
+PSUM_BANKS = 8
+QUADRANT = 32
+QUADRANTS = P // QUADRANT
+SCALE_ROWS = 4
+X_LOAD_CHUNKS = 2
+
+FLOPS = 2 * ROWS * PARTS * CHUNK * PARTS * CHUNK
+
+X_CHUNK = ((0, 1, 2, 3), (1, 0, 3, 2), (2, 3, 0, 1), (3, 2, 1, 0))
+SIGN = ((1, -1, -1, -1), (1, 1, -1, 1), (1, 1, 1, -1), (1, -1, 1, 1))
+
+OUT_PAIRS = ((0, 1), (2, 3))
+
+
+def tile_qdense_kernel(
+    tc,
+    x,
+    W_rr_words,
+    W_rr_scales,
+    W_ri_words,
+    W_ri_scales,
+    W_rj_words,
+    W_rj_scales,
+    W_rk_words,
+    W_rk_scales,
+    b_rr,
+    b_ri,
+    b_rj,
+    b_rk,
+    out,
+):
+    nc = tc.nc
+    words_in = (W_rr_words, W_ri_words, W_rj_words, W_rk_words)
+    scales_in = (W_rr_scales, W_ri_scales, W_rj_scales, W_rk_scales)
+    bias_in = (b_rr, b_ri, b_rj, b_rk)
+
+    with ExitStack() as ctx:
+        ctx.enter_context(tc.manual_schedule())
+        keep = ctx.enter_context(tc.tile_pool(name="keep", bufs=1))
+        x_pool = ctx.enter_context(tc.tile_pool(name="x_pool", bufs=ROW_BLOCKS * PARTS // X_LOAD_CHUNKS))
+        stage = ctx.enter_context(tc.tile_pool(name="stage", bufs=4))
+        psum = ctx.enter_context(tc.psum_pool(name="psum", bufs=PSUM_BANKS))
+
+        w_words = keep.tile([P, PARTS, COL_HALVES, PASSES, N_TILE], U32, align_bytes=64)
+        w_planes = keep.tile([P, PASSES, CHUNK], U8, align_bytes=64)
+        x_codes = keep.tile([P, ROW_BLOCKS, PARTS, PASSES, P], U32, align_bytes=64)
+        x_planes = keep.tile([P, ROW_BLOCKS, PARTS, PASSES, P], U8, align_bytes=64)
+        ident = keep.tile([P, P], F32)
+        bias_rows = keep.tile([P, CHUNK], BF16)
+        signs = keep.tile([P, PARTS, P], BF16)
+        bias_all = keep.tile([P, PARTS, CHUNK], F32)
+
+        nc.vector.memset(bias_rows[:].bitcast(I32), 0)
+        nc.vector.memset(w_planes[:].bitcast(I32), 0)
+        nc.vector.memset(signs[:], 1.0)
+        for o in range(PARTS):
+            for w in range(PARTS):
+                if SIGN[o][w] < 0:
+                    nc.vector.memset(signs[QUADRANT * w : QUADRANT * (w + 1), o, :], -1.0)
+        make_identity(nc, ident[:])
+
+        for w in range(PARTS):
+            nc.scalar.dma_start(
+                out=bias_rows[QUADRANT * w : QUADRANT * w + 1, :],
+                in_=bias_in[w].rearrange("(o n) -> o n", o=1),
+            )
+
+        def load_x(m):
+            loaded = []
+            for h in range(PARTS // X_LOAD_CHUNKS):
+                x_raw = x_pool.tile([P, X_LOAD_CHUNKS * CHUNK], BF16, tag="x_raw")
+                width = X_LOAD_CHUNKS * CHUNK
+                nc.sync.dma_start(out=x_raw[:], in_=x[P * m : P * (m + 1), width * h : width * (h + 1)])
+                loaded.append(x_raw)
+            return loaded
+
+        def load_scales(w):
+            for quad in range(QUADRANTS):
+                first = QUADRANT * quad + SCALE_ROWS * w
+                nc.sync.dma_start(
+                    out=w_planes[first : first + SCALE_ROWS, :, :].bitcast(I32),
+                    in_=scales_in[w][:, SCALE_ROWS * quad : SCALE_ROWS * (quad + 1), :]
+                    .rearrange("g r n -> r g n")
+                    .bitcast(I32),
+                )
+
+        def load_words(w, half):
+            byte_cols = slice(PACK * N_TILE * half, PACK * N_TILE * (half + 1))
+            nc.sync.dma_start(
+                out=w_words[:, w, half, :, :].bitcast(I32),
+                in_=words_in[w].rearrange("g p n t -> p g (n t)")[:, :, byte_cols].bitcast(I32),
+            )
+
+        x_raw_of = {0: load_x(0)}
+        for w in range(PARTS):
+            load_scales(w)
+            load_words(w, 0)
+        for w in range(PARTS):
+            load_words(w, 1)
+        x_raw_of[1] = load_x(1)
+
+        def spread_bias(half):
+            cols = slice(N_TILE * half, N_TILE * (half + 1))
+            for o in range(PARTS):
+                bank = psum.tile([P, N_TILE], F32, tag="bank")
+                nc.tensor.matmul(out=bank[:], lhsT=signs[:, o, :], rhs=bias_rows[:, cols], start=True, stop=True)
+                nc.scalar.copy(out=bias_all[:, o, cols], in_=bank[:])
+
+        def quantise_x(m):
+            for h in range(PARTS // X_LOAD_CHUNKS):
+                x_words = x_raw_of[m][h][:].bitcast(F32)
+                grouped = stage.tile([P, X_LOAD_CHUNKS, PASSES, P, PACK], BF16, tag="grouped", align_bytes=64)
+                for j in range(X_LOAD_CHUNKS):
+                    bank = psum.tile([P, N_TILE], F32, tag="bank")
+                    for g in range(PASSES):
+                        first = (K_PASS // 2) * (PASSES * j + g)
+                        for u in range(2):
+                            nc.tensor.transpose(
+                                bank[:].rearrange("p (g u r) -> p g u r", g=PASSES, u=2)[:, g, u, :],
+                                x_words[:, first + u : first + K_PASS // 2 : 2],
+                                ident[:],
+                            )
+                    copy = nc.vector.tensor_copy if j % 2 == 0 else nc.scalar.copy
+                    copy(
+                        out=grouped[:, j].bitcast(F32),
+                        in_=bank[:].rearrange("p (g u r) -> p g r u", g=PASSES, u=2),
+                    )
+                chunks = slice(X_LOAD_CHUNKS * h, X_LOAD_CHUNKS * (h + 1))
+                nc.vector.quantize_mx(
+                    out=x_codes[:, m, chunks].rearrange("p c g r -> p (c g r)").bitcast(FP8X4),
+                    scales=x_planes[:, m, chunks].rearrange("p c g r -> p (c g r)"),
+                    in_=grouped[:].rearrange("p c g r t -> p (c g r t)"),
+                )
+
+        def multiply(m, half, pair):
+            cols = slice(N_TILE * half, N_TILE * (half + 1))
+            banks = {}
+            for o in pair:
+                for sign in (1, -1):
+                    bank = psum.tile([P, N_TILE], F32, tag="bank")
+                    banks[(o, sign)] = bank
+            partial = {}
+            for w in range(PARTS):
+                for o in pair:
+                    sign = SIGN[o][w]
+                    same_sign = [v for v in range(PARTS) if SIGN[o][v] == sign]
+                    bank = banks[(o, sign)]
+                    for g in range(PASSES):
+                        nc.tensor.matmul_mx(
+                            out=bank[:],
+                            lhsT=x_codes[:, m, X_CHUNK[o][w], g, :].bitcast(FP8X4),
+                            lhsT_scale=x_planes[:, m, X_CHUNK[o][w], g, :],
+                            rhs=w_words[:, w, half, g, :].bitcast(FP8X4),
+                            rhs_scale=w_planes[SCALE_ROWS * w : P, g, cols],
+                            start=(w == same_sign[0] and g == 0),
+                            stop=(w == same_sign[-1] and g == PASSES - 1),
+                        )
+                    op = ALU.add if sign > 0 else ALU.subtract
+                    if w == same_sign[-1] and o not in partial:
+                        part = stage.tile([P, N_TILE], F32, tag="part")
+                        nc.vector.tensor_tensor(out=part[:], in0=bias_all[:, o, cols], in1=bank[:], op=op)
+                        partial[o] = part
+                    elif w == same_sign[-1]:
+                        result = stage.tile([P, N_TILE], F32, tag="result")
+                        nc.vector.tensor_tensor(out=result[:], in0=partial[o][:], in1=bank[:], op=op)
+                        first = CHUNK * o + N_TILE * half
+                        nc.sync.dma_start(out=out[P * m : P * (m + 1), first : first + N_TILE], in_=result[:])
+
+        quantise_x(0)
+        for half in range(COL_HALVES):
+            spread_bias(half)
+        for m in range(ROW_BLOCKS):
+            for half in range(COL_HALVES):
+                for pair in OUT_PAIRS:
+                    if m + 1 < ROW_BLOCKS and half == COL_HALVES - 1 and pair == OUT_PAIRS[-1]:
+                        quantise_x(m + 1)
+                    multiply(m, half, pair)

@@ -117,9 +117,9 @@ def tile_qdense_kernel(
         x_raw_of = {0: load_x(0)}
         for w in range(PARTS):
             load_scales(w)
-            load_words(w, 0)
-        for w in range(PARTS):
-            load_words(w, 1)
+        for half in range(COL_HALVES):
+            for w in range(PARTS):
+                load_words(w, half)
         x_raw_of[1] = load_x(1)
 
         def spread_bias(half):

@@ -32,7 +32,11 @@ FLOPS = 2 * ROWS * PARTS * CHUNK * PARTS * CHUNK
 X_CHUNK = ((0, 1, 2, 3), (1, 0, 3, 2), (2, 3, 0, 1), (3, 2, 1, 0))
 SIGN = ((1, -1, -1, -1), (1, 1, -1, 1), (1, 1, 1, -1), (1, -1, 1, 1))
 
-OUT_PAIRS = ((0, 1), (2, 3))
+WEIGHT_BY_WEIGHT = tuple((o, w) for w in range(PARTS) for o in range(PARTS))
+
+
+def weights_of(o):
+    return sorted(range(PARTS), key=lambda w: len([v for v in range(PARTS) if SIGN[o][v] == SIGN[o][w]]))
 
 
 def tile_qdense_kernel(
@@ -60,12 +64,20 @@ def tile_qdense_kernel(
     with ExitStack() as ctx:
         ctx.enter_context(tc.manual_schedule())
         keep = ctx.enter_context(tc.tile_pool(name="keep", bufs=1))
-        x_pool = ctx.enter_context(tc.tile_pool(name="x_pool", bufs=ROW_BLOCKS * PARTS // X_LOAD_CHUNKS))
+        x_pool = ctx.enter_context(tc.tile_pool(name="x_pool", bufs=ROW_BLOCKS * PARTS))
         stage = ctx.enter_context(tc.tile_pool(name="stage", bufs=4))
-        psum = ctx.enter_context(tc.psum_pool(name="psum", bufs=PSUM_BANKS))
+        psum = ctx.enter_context(tc.psum_pool(name="psum", bufs=1))
+
+        free_banks = list(range(PSUM_BANKS))
+
+        def take_bank():
+            number = free_banks[0]
+            free_banks.remove(number)
+            bank = psum.tile([P, N_TILE], F32, tag="bank%d" % number)
+            return number, bank
 
         w_words = keep.tile([P, PARTS, COL_HALVES, PASSES, N_TILE], U32, align_bytes=64)
-        w_planes = keep.tile([P, PASSES, CHUNK], U8, align_bytes=64)
+        w_planes = keep.tile([P, PARTS, PASSES, CHUNK], U8, align_bytes=64)
         x_codes = keep.tile([P, ROW_BLOCKS, PARTS, PASSES, P], U32, align_bytes=64)
         x_planes = keep.tile([P, ROW_BLOCKS, PARTS, PASSES, P], U8, align_bytes=64)
         ident = keep.tile([P, P], F32)
@@ -74,7 +86,8 @@ def tile_qdense_kernel(
         bias_all = keep.tile([P, PARTS, CHUNK], F32)
 
         nc.vector.memset(bias_rows[:].bitcast(I32), 0)
-        nc.vector.memset(w_planes[:].bitcast(I32), 0)
+        for w in range(PARTS):
+            nc.vector.memset(w_planes[:, w].bitcast(I32), 0)
         nc.vector.memset(signs[:], 1.0)
         for o in range(PARTS):
             for w in range(PARTS):
@@ -82,18 +95,11 @@ def tile_qdense_kernel(
                     nc.vector.memset(signs[QUADRANT * w : QUADRANT * (w + 1), o, :], -1.0)
         make_identity(nc, ident[:])
 
-        for w in range(PARTS):
-            nc.scalar.dma_start(
-                out=bias_rows[QUADRANT * w : QUADRANT * w + 1, :],
-                in_=bias_in[w].rearrange("(o n) -> o n", o=1),
-            )
-
         def load_x(m):
             loaded = []
-            for h in range(PARTS // X_LOAD_CHUNKS):
-                x_raw = x_pool.tile([P, X_LOAD_CHUNKS * CHUNK], BF16, tag="x_raw")
-                width = X_LOAD_CHUNKS * CHUNK
-                nc.sync.dma_start(out=x_raw[:], in_=x[P * m : P * (m + 1), width * h : width * (h + 1)])
+            for c in range(PARTS):
+                x_raw = x_pool.tile([P, CHUNK], BF16, tag="x_raw")
+                nc.sync.dma_start(out=x_raw[:], in_=x[P * m : P * (m + 1), CHUNK * c : CHUNK * (c + 1)])
                 loaded.append(x_raw)
             return loaded
 
@@ -101,7 +107,7 @@ def tile_qdense_kernel(
             for quad in range(QUADRANTS):
                 first = QUADRANT * quad + SCALE_ROWS * w
                 nc.sync.dma_start(
-                    out=w_planes[first : first + SCALE_ROWS, :, :].bitcast(I32),
+                    out=w_planes[first : first + SCALE_ROWS, w, :, :].bitcast(I32),
                     in_=scales_in[w][:, SCALE_ROWS * quad : SCALE_ROWS * (quad + 1), :]
                     .rearrange("g r n -> r g n")
                     .bitcast(I32),
@@ -116,27 +122,35 @@ def tile_qdense_kernel(
 
         x_raw_of = {0: load_x(0)}
         for w in range(PARTS):
+            nc.scalar.dma_start(
+                out=bias_rows[QUADRANT * w : QUADRANT * w + 1, :],
+                in_=bias_in[w].rearrange("(o n) -> o n", o=1),
+            )
+        for w in range(PARTS):
+            load_words(w, 0)
             load_scales(w)
-        for half in range(COL_HALVES):
-            for w in range(PARTS):
-                load_words(w, half)
+        for w in range(PARTS):
+            load_words(w, 1)
         x_raw_of[1] = load_x(1)
 
         def spread_bias(half):
             cols = slice(N_TILE * half, N_TILE * (half + 1))
             for o in range(PARTS):
-                bank = psum.tile([P, N_TILE], F32, tag="bank")
+                number, bank = take_bank()
                 nc.tensor.matmul(out=bank[:], lhsT=signs[:, o, :], rhs=bias_rows[:, cols], start=True, stop=True)
                 nc.scalar.copy(out=bias_all[:, o, cols], in_=bank[:])
+                free_banks.append(number)
 
         def quantise_x(m):
+            grouped_tiles = []
             for h in range(PARTS // X_LOAD_CHUNKS):
-                x_words = x_raw_of[m][h][:].bitcast(F32)
                 grouped = stage.tile([P, X_LOAD_CHUNKS, PASSES, P, PACK], BF16, tag="grouped", align_bytes=64)
+                grouped_tiles.append(grouped)
                 for j in range(X_LOAD_CHUNKS):
-                    bank = psum.tile([P, N_TILE], F32, tag="bank")
+                    x_words = x_raw_of[m][X_LOAD_CHUNKS * h + j][:].bitcast(F32)
+                    number, bank = take_bank()
                     for g in range(PASSES):
-                        first = (K_PASS // 2) * (PASSES * j + g)
+                        first = (K_PASS // 2) * g
                         for u in range(2):
                             nc.tensor.transpose(
                                 bank[:].rearrange("p (g u r) -> p g u r", g=PASSES, u=2)[:, g, u, :],
@@ -148,53 +162,63 @@ def tile_qdense_kernel(
                         out=grouped[:, j].bitcast(F32),
                         in_=bank[:].rearrange("p (g u r) -> p g r u", g=PASSES, u=2),
                     )
+                    free_banks.append(number)
+            for h in range(PARTS // X_LOAD_CHUNKS):
                 chunks = slice(X_LOAD_CHUNKS * h, X_LOAD_CHUNKS * (h + 1))
                 nc.vector.quantize_mx(
                     out=x_codes[:, m, chunks].rearrange("p c g r -> p (c g r)").bitcast(FP8X4),
                     scales=x_planes[:, m, chunks].rearrange("p c g r -> p (c g r)"),
-                    in_=grouped[:].rearrange("p c g r t -> p (c g r t)"),
+                    in_=grouped_tiles[h][:].rearrange("p c g r t -> p (c g r t)"),
                 )
 
-        def multiply(m, half, pair):
+        def multiply(m, half, order):
             cols = slice(N_TILE * half, N_TILE * (half + 1))
-            banks = {}
-            for o in pair:
-                for sign in (1, -1):
-                    bank = psum.tile([P, N_TILE], F32, tag="bank")
-                    banks[(o, sign)] = bank
+            groups = {}
+            taken = {}
             partial = {}
-            for w in range(PARTS):
-                for o in pair:
-                    sign = SIGN[o][w]
-                    same_sign = [v for v in range(PARTS) if SIGN[o][v] == sign]
-                    bank = banks[(o, sign)]
-                    for g in range(PASSES):
-                        nc.tensor.matmul_mx(
-                            out=bank[:],
-                            lhsT=x_codes[:, m, X_CHUNK[o][w], g, :].bitcast(FP8X4),
-                            lhsT_scale=x_planes[:, m, X_CHUNK[o][w], g, :],
-                            rhs=w_words[:, w, half, g, :].bitcast(FP8X4),
-                            rhs_scale=w_planes[SCALE_ROWS * w : P, g, cols],
-                            start=(w == same_sign[0] and g == 0),
-                            stop=(w == same_sign[-1] and g == PASSES - 1),
-                        )
-                    op = ALU.add if sign > 0 else ALU.subtract
-                    if w == same_sign[-1] and o not in partial:
-                        part = stage.tile([P, N_TILE], F32, tag="part")
-                        nc.vector.tensor_tensor(out=part[:], in0=bias_all[:, o, cols], in1=bank[:], op=op)
-                        partial[o] = part
-                    elif w == same_sign[-1]:
-                        result = stage.tile([P, N_TILE], F32, tag="result")
-                        nc.vector.tensor_tensor(out=result[:], in0=partial[o][:], in1=bank[:], op=op)
-                        first = CHUNK * o + N_TILE * half
-                        nc.sync.dma_start(out=out[P * m : P * (m + 1), first : first + N_TILE], in_=result[:])
+            for o, w in order:
+                sign = SIGN[o][w]
+                members = len([v for v in range(PARTS) if SIGN[o][v] == sign])
+                if (o, sign) not in groups:
+                    groups[(o, sign)] = take_bank()
+                    taken[(o, sign)] = 0
+                number, bank = groups[(o, sign)]
+                opens = taken[(o, sign)] == 0
+                taken[(o, sign)] = taken[(o, sign)] + 1
+                closes = taken[(o, sign)] == members
+                for g in range(PASSES):
+                    nc.tensor.matmul_mx(
+                        out=bank[:],
+                        lhsT=x_codes[:, m, X_CHUNK[o][w], g, :].bitcast(FP8X4),
+                        lhsT_scale=x_planes[:, m, X_CHUNK[o][w], g, :],
+                        rhs=w_words[:, w, half, g, :].bitcast(FP8X4),
+                        rhs_scale=w_planes[SCALE_ROWS * w : P, w, g, cols],
+                        start=(opens and g == 0),
+                        stop=(closes and g == PASSES - 1),
+                    )
+                if not closes:
+                    continue
+                op = ALU.add if sign > 0 else ALU.subtract
+                if o not in partial:
+                    part = stage.tile([P, N_TILE], F32, tag="part")
+                    nc.vector.tensor_tensor(out=part[:], in0=bias_all[:, o, cols], in1=bank[:], op=op)
+                    partial[o] = part
+                else:
+                    result = stage.tile([P, N_TILE], F32, tag="result")
+                    nc.vector.tensor_tensor(out=result[:], in0=partial[o][:], in1=bank[:], op=op)
+                    first = CHUNK * o + N_TILE * half
+                    nc.sync.dma_start(out=out[P * m : P * (m + 1), first : first + N_TILE], in_=result[:])
+                free_banks.append(number)
+
+        def chunk_by_chunk(chunks):
+            return [(o, w) for o in chunks for w in weights_of(o)]
 
         quantise_x(0)
         for half in range(COL_HALVES):
             spread_bias(half)
-        for m in range(ROW_BLOCKS):
-            for half in range(COL_HALVES):
-                for pair in OUT_PAIRS:
-                    if m + 1 < ROW_BLOCKS and half == COL_HALVES - 1 and pair == OUT_PAIRS[-1]:
-                        quantise_x(m + 1)
-                    multiply(m, half, pair)
+        multiply(0, 0, WEIGHT_BY_WEIGHT)
+        multiply(0, 1, chunk_by_chunk((0, 1)))
+        quantise_x(1)
+        multiply(0, 1, chunk_by_chunk((2, 3)))
+        for half in range(COL_HALVES):
+            multiply(1, half, chunk_by_chunk(range(PARTS)))

@@ -33,6 +33,7 @@ X_CHUNK = ((0, 1, 2, 3), (1, 0, 3, 2), (2, 3, 0, 1), (3, 2, 1, 0))
 SIGN = ((1, -1, -1, -1), (1, 1, -1, 1), (1, 1, 1, -1), (1, -1, 1, 1))
 
 WEIGHT_BY_WEIGHT = tuple((o, w) for w in range(PARTS) for o in range(PARTS))
+PAIR_BY_PAIR = tuple((o, w) for pair in ((0, 1), (2, 3)) for w in range(PARTS) for o in pair)
 
 
 def weights_of(o):
@@ -171,12 +172,14 @@ def tile_qdense_kernel(
                     in_=grouped_tiles[h][:].rearrange("p c g r t -> p (c g r t)"),
                 )
 
-        def multiply(m, half, order):
+        def multiply(m, half, order, next_x_before=None):
             cols = slice(N_TILE * half, N_TILE * (half + 1))
             groups = {}
             taken = {}
             partial = {}
-            for o, w in order:
+            for position, (o, w) in enumerate(order):
+                if position == next_x_before:
+                    quantise_x(m + 1)
                 sign = SIGN[o][w]
                 members = len([v for v in range(PARTS) if SIGN[o][v] == sign])
                 if (o, sign) not in groups:
@@ -217,8 +220,6 @@ def tile_qdense_kernel(
         for half in range(COL_HALVES):
             spread_bias(half)
         multiply(0, 0, WEIGHT_BY_WEIGHT)
-        multiply(0, 1, chunk_by_chunk((0, 1)))
-        quantise_x(1)
-        multiply(0, 1, chunk_by_chunk((2, 3)))
+        multiply(0, 1, PAIR_BY_PAIR, next_x_before=len(PAIR_BY_PAIR) - PARTS)
         for half in range(COL_HALVES):
             multiply(1, half, chunk_by_chunk(range(PARTS)))

@@ -26,6 +26,7 @@ QUADRANT = 32
 QUADRANTS = P // QUADRANT
 SCALE_ROWS = 4
 X_LOAD_CHUNKS = 2
+LAST_WIDTHS = (256, 256)
 
 FLOPS = 2 * ROWS * PARTS * CHUNK * PARTS * CHUNK
 
@@ -142,20 +143,37 @@ def tile_qdense_kernel(
                 nc.scalar.copy(out=bias_all[:, o, cols], in_=bank[:])
                 free_banks.append(number)
 
+        x_sorted_of = {}
+
+        def sort_x(m):
+            x_sorted_of[m] = []
+            for c in range(PARTS):
+                x_sorted = x_pool.tile([P, PASSES, 2, P], F32, tag="x_sorted")
+                nc.scalar.copy(
+                    out=x_sorted[:],
+                    in_=x_raw_of[m][c][:].bitcast(F32).rearrange("p (g i u) -> p g u i", g=PASSES, u=2),
+                )
+                x_sorted_of[m].append(x_sorted)
+
         def quantise_x(m):
             grouped_tiles = []
             for h in range(PARTS // X_LOAD_CHUNKS):
                 grouped = stage.tile([P, X_LOAD_CHUNKS, PASSES, P, PACK], BF16, tag="grouped", align_bytes=64)
                 grouped_tiles.append(grouped)
                 for j in range(X_LOAD_CHUNKS):
-                    x_words = x_raw_of[m][X_LOAD_CHUNKS * h + j][:].bitcast(F32)
+                    c = X_LOAD_CHUNKS * h + j
+                    x_words = x_raw_of[m][c][:].bitcast(F32)
                     number, bank = take_bank()
                     for g in range(PASSES):
                         first = (K_PASS // 2) * g
                         for u in range(2):
+                            if m in x_sorted_of:
+                                words = x_sorted_of[m][c][:, g, u, :]
+                            else:
+                                words = x_words[:, first + u : first + K_PASS // 2 : 2]
                             nc.tensor.transpose(
                                 bank[:].rearrange("p (g u r) -> p g u r", g=PASSES, u=2)[:, g, u, :],
-                                x_words[:, first + u : first + K_PASS // 2 : 2],
+                                words,
                                 ident[:],
                             )
                     copy = nc.vector.tensor_copy if j % 2 == 0 else nc.scalar.copy
@@ -172,8 +190,9 @@ def tile_qdense_kernel(
                     in_=grouped_tiles[h][:].rearrange("p c g r t -> p (c g r t)"),
                 )
 
-        def multiply(m, half, order, next_x_before=None):
-            cols = slice(N_TILE * half, N_TILE * (half + 1))
+        def multiply(m, half, order, next_x_before=None, first=0, width=N_TILE):
+            inner = slice(first, first + width)
+            cols = slice(N_TILE * half + first, N_TILE * half + first + width)
             groups = {}
             taken = {}
             partial = {}
@@ -191,10 +210,10 @@ def tile_qdense_kernel(
                 closes = taken[(o, sign)] == members
                 for g in range(PASSES):
                     nc.tensor.matmul_mx(
-                        out=bank[:],
+                        out=bank[:, 0:width],
                         lhsT=x_codes[:, m, X_CHUNK[o][w], g, :].bitcast(FP8X4),
                         lhsT_scale=x_planes[:, m, X_CHUNK[o][w], g, :],
-                        rhs=w_words[:, w, half, g, :].bitcast(FP8X4),
+                        rhs=w_words[:, w, half, g, inner].bitcast(FP8X4),
                         rhs_scale=w_planes[SCALE_ROWS * w : P, w, g, cols],
                         start=(opens and g == 0),
                         stop=(closes and g == PASSES - 1),
@@ -203,14 +222,15 @@ def tile_qdense_kernel(
                     continue
                 op = ALU.add if sign > 0 else ALU.subtract
                 if o not in partial:
-                    part = stage.tile([P, N_TILE], F32, tag="part")
-                    nc.vector.tensor_tensor(out=part[:], in0=bias_all[:, o, cols], in1=bank[:], op=op)
+                    part = stage.tile([P, width], F32, tag="part")
+                    nc.vector.tensor_tensor(out=part[:], in0=bias_all[:, o, cols], in1=bank[:, 0:width], op=op)
                     partial[o] = part
                 else:
-                    result = stage.tile([P, N_TILE], F32, tag="result")
-                    nc.vector.tensor_tensor(out=result[:], in0=partial[o][:], in1=bank[:], op=op)
-                    first = CHUNK * o + N_TILE * half
-                    nc.sync.dma_start(out=out[P * m : P * (m + 1), first : first + N_TILE], in_=result[:])
+                    result = stage.tile([P, width], F32, tag="result")
+                    nc.vector.tensor_tensor(out=result[:], in0=partial[o][:], in1=bank[:, 0:width], op=op)
+                    nc.sync.dma_start(
+                        out=out[P * m : P * (m + 1), CHUNK * o + cols.start : CHUNK * o + cols.stop], in_=result[:]
+                    )
                 free_banks.append(number)
 
         def chunk_by_chunk(chunks):
@@ -220,6 +240,11 @@ def tile_qdense_kernel(
         for half in range(COL_HALVES):
             spread_bias(half)
         multiply(0, 0, WEIGHT_BY_WEIGHT)
+        sort_x(1)
         multiply(0, 1, PAIR_BY_PAIR, next_x_before=len(PAIR_BY_PAIR) - PARTS)
-        for half in range(COL_HALVES):
-            multiply(1, half, chunk_by_chunk(range(PARTS)))
+        multiply(1, 0, chunk_by_chunk(range(PARTS)))
+        multiply(1, 1, chunk_by_chunk(range(PARTS - 1)))
+        first = 0
+        for width in LAST_WIDTHS:
+            multiply(1, 1, chunk_by_chunk((PARTS - 1,)), first=first, width=width)
+            first += width

@@ -87,7 +87,7 @@ def tile_qdense_kernel(
         signs = keep.tile([P, PARTS, P], BF16)
         bias_all = keep.tile([P, PARTS, CHUNK], F32)
 
-        nc.vector.memset(bias_rows[:].bitcast(I32), 0)
+        nc.gpsimd.memset(bias_rows[:].bitcast(F32), 0.0)
         for w in range(PARTS):
             nc.vector.memset(w_planes[:, w].bitcast(I32), 0)
         nc.vector.memset(signs[:], 1.0)
@@ -97,13 +97,16 @@ def tile_qdense_kernel(
                     nc.vector.memset(signs[QUADRANT * w : QUADRANT * (w + 1), o, :], -1.0)
         make_identity(nc, ident[:])
 
-        def load_x(m):
-            loaded = []
-            for c in range(PARTS):
-                x_raw = x_pool.tile([P, CHUNK], BF16, tag="x_raw")
-                nc.sync.dma_start(out=x_raw[:], in_=x[P * m : P * (m + 1), CHUNK * c : CHUNK * (c + 1)])
-                loaded.append(x_raw)
-            return loaded
+        def load_x(m, loads):
+            words = {}
+            for chunks in loads:
+                x_raw = x_pool.tile([P, CHUNK * len(chunks)], BF16, tag="x_raw")
+                nc.sync.dma_start(
+                    out=x_raw[:], in_=x[P * m : P * (m + 1), CHUNK * chunks[0] : CHUNK * (chunks[-1] + 1)]
+                )
+                for i, c in enumerate(chunks):
+                    words[c] = x_raw[:, CHUNK * i : CHUNK * (i + 1)].bitcast(F32)
+            return words
 
         def load_scales(w):
             for quad in range(QUADRANTS):
@@ -122,18 +125,19 @@ def tile_qdense_kernel(
                 in_=words_in[w].rearrange("g p n t -> p g (n t)")[:, :, byte_cols].bitcast(I32),
             )
 
-        x_raw_of = {0: load_x(0)}
+        x_words_of = {0: load_x(0, ((0,), (1,)))}
         for w in range(PARTS):
-            nc.scalar.dma_start(
+            nc.sync.dma_start(
                 out=bias_rows[QUADRANT * w : QUADRANT * w + 1, :],
                 in_=bias_in[w].rearrange("(o n) -> o n", o=1),
             )
+        x_words_of[0].update(load_x(0, ((2, 3),)))
         for w in range(PARTS):
             load_words(w, 0)
             load_scales(w)
         for w in range(PARTS):
             load_words(w, 1)
-        x_raw_of[1] = load_x(1)
+        x_words_of[1] = load_x(1, ((0, 1), (2, 3)))
 
         def spread_bias(half):
             cols = slice(N_TILE * half, N_TILE * (half + 1))
@@ -151,44 +155,48 @@ def tile_qdense_kernel(
                 x_sorted = x_pool.tile([P, PASSES, 2, P], F32, tag="x_sorted")
                 nc.scalar.copy(
                     out=x_sorted[:],
-                    in_=x_raw_of[m][c][:].bitcast(F32).rearrange("p (g i u) -> p g u i", g=PASSES, u=2),
+                    in_=x_words_of[m][c].rearrange("p (g i u) -> p g u i", g=PASSES, u=2),
                 )
                 x_sorted_of[m].append(x_sorted)
 
-        def quantise_x(m):
-            grouped_tiles = []
-            for h in range(PARTS // X_LOAD_CHUNKS):
-                grouped = stage.tile([P, X_LOAD_CHUNKS, PASSES, P, PACK], BF16, tag="grouped", align_bytes=64)
-                grouped_tiles.append(grouped)
-                for j in range(X_LOAD_CHUNKS):
-                    c = X_LOAD_CHUNKS * h + j
-                    x_words = x_raw_of[m][c][:].bitcast(F32)
-                    number, bank = take_bank()
-                    for g in range(PASSES):
-                        first = (K_PASS // 2) * g
-                        for u in range(2):
-                            if m in x_sorted_of:
-                                words = x_sorted_of[m][c][:, g, u, :]
-                            else:
-                                words = x_words[:, first + u : first + K_PASS // 2 : 2]
-                            nc.tensor.transpose(
-                                bank[:].rearrange("p (g u r) -> p g u r", g=PASSES, u=2)[:, g, u, :],
-                                words,
-                                ident[:],
-                            )
-                    copy = nc.vector.tensor_copy if j % 2 == 0 else nc.scalar.copy
-                    copy(
-                        out=grouped[:, j].bitcast(F32),
-                        in_=bank[:].rearrange("p (g u r) -> p g r u", g=PASSES, u=2),
-                    )
-                    free_banks.append(number)
-            for h in range(PARTS // X_LOAD_CHUNKS):
-                chunks = slice(X_LOAD_CHUNKS * h, X_LOAD_CHUNKS * (h + 1))
-                nc.vector.quantize_mx(
-                    out=x_codes[:, m, chunks].rearrange("p c g r -> p (c g r)").bitcast(FP8X4),
-                    scales=x_planes[:, m, chunks].rearrange("p c g r -> p (c g r)"),
-                    in_=grouped_tiles[h][:].rearrange("p c g r t -> p (c g r t)"),
+        def transpose_pair(m, h):
+            grouped = stage.tile([P, X_LOAD_CHUNKS, PASSES, P, PACK], BF16, tag="grouped", align_bytes=64)
+            for j in range(X_LOAD_CHUNKS):
+                c = X_LOAD_CHUNKS * h + j
+                number, bank = take_bank()
+                for g in range(PASSES):
+                    first = (K_PASS // 2) * g
+                    for u in range(2):
+                        if m in x_sorted_of:
+                            words = x_sorted_of[m][c][:, g, u, :]
+                        else:
+                            words = x_words_of[m][c][:, first + u : first + K_PASS // 2 : 2]
+                        nc.tensor.transpose(
+                            bank[:].rearrange("p (g u r) -> p g u r", g=PASSES, u=2)[:, g, u, :],
+                            words,
+                            ident[:],
+                        )
+                copy = nc.vector.tensor_copy if j % 2 == 0 else nc.scalar.copy
+                copy(
+                    out=grouped[:, j].bitcast(F32),
+                    in_=bank[:].rearrange("p (g u r) -> p g r u", g=PASSES, u=2),
                 )
+                free_banks.append(number)
+            return grouped
+
+        def quantise_pair(m, h, grouped):
+            chunks = slice(X_LOAD_CHUNKS * h, X_LOAD_CHUNKS * (h + 1))
+            nc.vector.quantize_mx(
+                out=x_codes[:, m, chunks].rearrange("p c g r -> p (c g r)").bitcast(FP8X4),
+                scales=x_planes[:, m, chunks].rearrange("p c g r -> p (c g r)"),
+                in_=grouped[:].rearrange("p c g r t -> p (c g r t)"),
+            )
+
+        def quantise_x(m):
+            pairs = range(PARTS // X_LOAD_CHUNKS)
+            grouped_tiles = [transpose_pair(m, h) for h in pairs]
+            for h in pairs:
+                quantise_pair(m, h, grouped_tiles[h])
 
         def multiply(m, half, order, next_x_before=None, first=0, width=N_TILE):
             inner = slice(first, first + width)
@@ -236,9 +244,10 @@ def tile_qdense_kernel(
         def chunk_by_chunk(chunks):
             return [(o, w) for o in chunks for w in weights_of(o)]
 
-        quantise_x(0)
-        for half in range(COL_HALVES):
-            spread_bias(half)
+        for h in range(PARTS // X_LOAD_CHUNKS):
+            grouped = transpose_pair(0, h)
+            spread_bias(h)
+            quantise_pair(0, h, grouped)
         multiply(0, 0, WEIGHT_BY_WEIGHT)
         sort_x(1)
         multiply(0, 1, PAIR_BY_PAIR, next_x_before=len(PAIR_BY_PAIR) - PARTS)

@@ -139,11 +139,19 @@ def tile_qdense_kernel(
             load_words(w, 1)
         x_words_of[1] = load_x(1, ((0, 1), (2, 3)))
 
-        def spread_bias(half):
+        def bias_matmuls(half):
             cols = slice(N_TILE * half, N_TILE * (half + 1))
+            filled = []
             for o in range(PARTS):
                 number, bank = take_bank()
                 nc.tensor.matmul(out=bank[:], lhsT=signs[:, o, :], rhs=bias_rows[:, cols], start=True, stop=True)
+                filled.append((number, bank))
+            return filled
+
+        def bias_copies(half, filled, chunks):
+            cols = slice(N_TILE * half, N_TILE * (half + 1))
+            for o in chunks:
+                number, bank = filled[o]
                 nc.scalar.copy(out=bias_all[:, o, cols], in_=bank[:])
                 free_banks.append(number)
 
@@ -198,61 +206,72 @@ def tile_qdense_kernel(
             for h in pairs:
                 quantise_pair(m, h, grouped_tiles[h])
 
-        def multiply(m, half, order, next_x_before=None, first=0, width=N_TILE):
+        def multiply(m, half, order, together=1, next_x_before=None, first=0, width=N_TILE):
             inner = slice(first, first + width)
             cols = slice(N_TILE * half + first, N_TILE * half + first + width)
             groups = {}
             taken = {}
             partial = {}
-            for position, (o, w) in enumerate(order):
+            for position in range(0, len(order), together):
                 if position == next_x_before:
                     quantise_x(m + 1)
-                sign = SIGN[o][w]
-                members = len([v for v in range(PARTS) if SIGN[o][v] == sign])
-                if (o, sign) not in groups:
-                    groups[(o, sign)] = take_bank()
-                    taken[(o, sign)] = 0
-                number, bank = groups[(o, sign)]
-                opens = taken[(o, sign)] == 0
-                taken[(o, sign)] = taken[(o, sign)] + 1
-                closes = taken[(o, sign)] == members
+                step = []
+                for o, w in order[position : position + together]:
+                    sign = SIGN[o][w]
+                    members = len([v for v in range(PARTS) if SIGN[o][v] == sign])
+                    if (o, sign) not in groups:
+                        groups[(o, sign)] = take_bank()
+                        taken[(o, sign)] = 0
+                    number, bank = groups[(o, sign)]
+                    opens = taken[(o, sign)] == 0
+                    taken[(o, sign)] = taken[(o, sign)] + 1
+                    closes = taken[(o, sign)] == members
+                    step.append((o, w, sign, number, bank, opens, closes))
                 for g in range(PASSES):
-                    nc.tensor.matmul_mx(
-                        out=bank[:, 0:width],
-                        lhsT=x_codes[:, m, X_CHUNK[o][w], g, :].bitcast(FP8X4),
-                        lhsT_scale=x_planes[:, m, X_CHUNK[o][w], g, :],
-                        rhs=w_words[:, w, half, g, inner].bitcast(FP8X4),
-                        rhs_scale=w_planes[SCALE_ROWS * w : P, w, g, cols],
-                        start=(opens and g == 0),
-                        stop=(closes and g == PASSES - 1),
-                    )
-                if not closes:
-                    continue
-                op = ALU.add if sign > 0 else ALU.subtract
-                if o not in partial:
-                    part = stage.tile([P, width], F32, tag="part")
-                    nc.vector.tensor_tensor(out=part[:], in0=bias_all[:, o, cols], in1=bank[:, 0:width], op=op)
-                    partial[o] = part
-                else:
-                    result = stage.tile([P, width], F32, tag="result")
-                    nc.vector.tensor_tensor(out=result[:], in0=partial[o][:], in1=bank[:, 0:width], op=op)
-                    nc.sync.dma_start(
-                        out=out[P * m : P * (m + 1), CHUNK * o + cols.start : CHUNK * o + cols.stop], in_=result[:]
-                    )
-                free_banks.append(number)
+                    for o, w, sign, number, bank, opens, closes in step:
+                        nc.tensor.matmul_mx(
+                            out=bank[:, 0:width],
+                            lhsT=x_codes[:, m, X_CHUNK[o][w], g, :].bitcast(FP8X4),
+                            lhsT_scale=x_planes[:, m, X_CHUNK[o][w], g, :],
+                            rhs=w_words[:, w, half, g, inner].bitcast(FP8X4),
+                            rhs_scale=w_planes[SCALE_ROWS * w : P, w, g, cols],
+                            start=(opens and g == 0),
+                            stop=(closes and g == PASSES - 1),
+                        )
+                for o, w, sign, number, bank, opens, closes in step:
+                    if not closes:
+                        continue
+                    op = ALU.add if sign > 0 else ALU.subtract
+                    if o not in partial:
+                        part = stage.tile([P, width], F32, tag="part")
+                        nc.vector.tensor_tensor(out=part[:], in0=bias_all[:, o, cols], in1=bank[:, 0:width], op=op)
+                        partial[o] = part
+                    else:
+                        result = stage.tile([P, width], F32, tag="result")
+                        nc.vector.tensor_tensor(out=result[:], in0=partial[o][:], in1=bank[:, 0:width], op=op)
+                        nc.sync.dma_start(
+                            out=out[P * m : P * (m + 1), CHUNK * o + cols.start : CHUNK * o + cols.stop],
+                            in_=result[:],
+                        )
+                    free_banks.append(number)
 
         def chunk_by_chunk(chunks):
             return [(o, w) for o in chunks for w in weights_of(o)]
 
-        for h in range(PARTS // X_LOAD_CHUNKS):
-            grouped = transpose_pair(0, h)
-            spread_bias(h)
-            quantise_pair(0, h, grouped)
-        multiply(0, 0, WEIGHT_BY_WEIGHT)
+        grouped = transpose_pair(0, 0)
+        filled = bias_matmuls(0)
+        bias_copies(0, filled, (0, 1))
+        quantise_pair(0, 0, grouped)
+        grouped = transpose_pair(0, 1)
+        bias_copies(0, filled, (2, 3))
+        quantise_pair(0, 1, grouped)
+        bias_copies(1, bias_matmuls(1), range(PARTS))
+        multiply(0, 0, WEIGHT_BY_WEIGHT, together=2)
         sort_x(1)
-        multiply(0, 1, PAIR_BY_PAIR, next_x_before=len(PAIR_BY_PAIR) - PARTS)
-        multiply(1, 0, chunk_by_chunk(range(PARTS)))
-        multiply(1, 1, chunk_by_chunk(range(PARTS - 1)))
+        multiply(0, 1, PAIR_BY_PAIR, together=2, next_x_before=len(PAIR_BY_PAIR) - PARTS)
+        multiply(1, 0, PAIR_BY_PAIR, together=2)
+        multiply(1, 1, PAIR_BY_PAIR[: len(PAIR_BY_PAIR) // 2], together=2)
+        multiply(1, 1, chunk_by_chunk((PARTS - 2,)))
         first = 0
         for width in LAST_WIDTHS:
             multiply(1, 1, chunk_by_chunk((PARTS - 1,)), first=first, width=width)

@@ -26,6 +26,7 @@ QUADRANT = 32
 QUADRANTS = P // QUADRANT
 SCALE_ROWS = 4
 X_LOAD_CHUNKS = 2
+WARM_UP = 5
 LAST_WIDTHS = (256, 256)
 
 FLOPS = 2 * ROWS * PARTS * CHUNK * PARTS * CHUNK
@@ -87,6 +88,8 @@ def tile_qdense_kernel(
         signs = keep.tile([P, PARTS, P], BF16)
         bias_all = keep.tile([P, PARTS, CHUNK], F32)
 
+        warm = keep.tile([P, N_TILE], BF16)
+        nc.gpsimd.memset(warm[:].bitcast(F32), 0.0)
         nc.gpsimd.memset(bias_rows[:].bitcast(F32), 0.0)
         for w in range(PARTS):
             nc.vector.memset(w_planes[:, w].bitcast(I32), 0)
@@ -258,6 +261,10 @@ def tile_qdense_kernel(
         def chunk_by_chunk(chunks):
             return [(o, w) for o in chunks for w in weights_of(o)]
 
+        for i in range(WARM_UP):
+            number, bank = take_bank()
+            nc.tensor.matmul(out=bank[:], lhsT=warm[:, 0:P], rhs=warm[:], start=True, stop=True)
+            free_banks.append(number)
         grouped = transpose_pair(0, 0)
         filled = bias_matmuls(0)
         bias_copies(0, filled, (0, 1))

@@ -80,7 +80,7 @@ def tile_qdense_kernel(
             return number, bank
 
         w_words = keep.tile([P, PARTS, COL_HALVES, PASSES, N_TILE], U32, align_bytes=64)
-        w_planes = keep.tile([P, PARTS, PASSES, CHUNK], U8, align_bytes=64)
+        w_planes = keep.tile([P, PARTS, CHUNK], U8, align_bytes=64)
         x_codes = keep.tile([P, ROW_BLOCKS, PARTS, PASSES, P], U32, align_bytes=64)
         x_planes = keep.tile([P, ROW_BLOCKS, PARTS, PASSES, P], U8, align_bytes=64)
         ident = keep.tile([P, P], F32)
@@ -113,12 +113,10 @@ def tile_qdense_kernel(
 
         def load_scales(w):
             for quad in range(QUADRANTS):
-                first = QUADRANT * quad + SCALE_ROWS * w
+                first = QUADRANT * quad
                 nc.sync.dma_start(
-                    out=w_planes[first : first + SCALE_ROWS, w, :, :].bitcast(I32),
-                    in_=scales_in[w][:, SCALE_ROWS * quad : SCALE_ROWS * (quad + 1), :]
-                    .rearrange("g r n -> r g n")
-                    .bitcast(I32),
+                    out=w_planes[first : first + PASSES * SCALE_ROWS, w, :].bitcast(I32),
+                    in_=scales_in[w][:, SCALE_ROWS * quad : SCALE_ROWS * (quad + 1), :].bitcast(I32),
                 )
 
         def load_words(w, half):
@@ -237,7 +235,7 @@ def tile_qdense_kernel(
                             lhsT=x_codes[:, m, X_CHUNK[o][w], g, :].bitcast(FP8X4),
                             lhsT_scale=x_planes[:, m, X_CHUNK[o][w], g, :],
                             rhs=w_words[:, w, half, g, inner].bitcast(FP8X4),
-                            rhs_scale=w_planes[SCALE_ROWS * w : P, w, g, cols],
+                            rhs_scale=w_planes[SCALE_ROWS * g : P, w, cols],
                             start=(opens and g == 0),
                             stop=(closes and g == PASSES - 1),
                         )

@@ -24,6 +24,7 @@ COL_HALVES = CHUNK // N_TILE
 PSUM_BANKS = 8
 QUADRANT = 32
 QUADRANTS = P // QUADRANT
+PIECES = CHUNK // QUADRANT
 SCALE_ROWS = 4
 X_LOAD_CHUNKS = 2
 WARM_UP = 5
@@ -34,8 +35,11 @@ FLOPS = 2 * ROWS * PARTS * CHUNK * PARTS * CHUNK
 X_CHUNK = ((0, 1, 2, 3), (1, 0, 3, 2), (2, 3, 0, 1), (3, 2, 1, 0))
 SIGN = ((1, -1, -1, -1), (1, 1, -1, 1), (1, 1, 1, -1), (1, -1, 1, 1))
 
-WEIGHT_BY_WEIGHT = tuple((o, w) for w in range(PARTS) for o in range(PARTS))
-PAIR_BY_PAIR = tuple((o, w) for pair in ((0, 1), (2, 3)) for w in range(PARTS) for o in pair)
+HEAD = (((0, 0),), ((1, 0),), ((0, 1), (1, 1)))
+FIRST_ROUND = HEAD + (((2, 0), (3, 0)), ((2, 1), (3, 1))) + tuple(
+    ((o, w), (o + 1, w)) for w in range(2, PARTS) for o in range(0, PARTS, 2)
+)
+PAIR_BY_PAIR = tuple(tuple((o, w) for o in pair) for pair in ((0, 1), (2, 3)) for w in range(PARTS))
 
 
 def weights_of(o):
@@ -84,21 +88,33 @@ def tile_qdense_kernel(
         x_codes = keep.tile([P, ROW_BLOCKS, PARTS, PASSES, P], U32, align_bytes=64)
         x_planes = keep.tile([P, ROW_BLOCKS, PARTS, PASSES, P], U8, align_bytes=64)
         ident = keep.tile([P, P], F32)
-        bias_rows = keep.tile([P, CHUNK], BF16)
-        signs = keep.tile([P, PARTS, P], BF16)
-        bias_all = keep.tile([P, PARTS, CHUNK], F32)
+        bias_pieces = keep.tile([P, QUADRANT], BF16)
+        bias_lhs = keep.tile([P, QUADRANTS, QUADRANT], BF16)
+        signs = keep.tile([P, PARTS], F32)
+        select = keep.tile([P, PARTS, QUADRANT], BF16)
+        bias_cols = keep.tile([P, PARTS, PIECES], F32)
+        bias_wide = keep.tile([P, PARTS, PIECES, QUADRANT], F32, align_bytes=64)
+        bias_all = keep.tile([P, PARTS, CHUNK], F32, align_bytes=64)
 
         warm = keep.tile([P, N_TILE], BF16)
         nc.gpsimd.memset(warm[:].bitcast(F32), 0.0)
-        nc.gpsimd.memset(bias_rows[:].bitcast(F32), 0.0)
         for w in range(PARTS):
             nc.vector.memset(w_planes[:, w].bitcast(I32), 0)
-        nc.vector.memset(signs[:], 1.0)
+        make_identity(nc, ident[:])
+        nc.gpsimd.memset(signs[:], 1.0)
         for o in range(PARTS):
             for w in range(PARTS):
                 if SIGN[o][w] < 0:
-                    nc.vector.memset(signs[QUADRANT * w : QUADRANT * (w + 1), o, :], -1.0)
-        make_identity(nc, ident[:])
+                    nc.gpsimd.memset(signs[QUADRANT * w : QUADRANT * (w + 1), o : o + 1], -1.0)
+        for w in range(PARTS):
+            rows = slice(QUADRANT * w, QUADRANT * (w + 1))
+            shape = [QUADRANT, PARTS, QUADRANT]
+            nc.gpsimd.tensor_tensor(
+                out=select[rows],
+                in0=ident[rows, rows].unsqueeze(1).to_broadcast(shape),
+                in1=signs[rows].unsqueeze(2).to_broadcast(shape),
+                op=ALU.mult,
+            )
 
         def load_x(m, loads):
             words = {}
@@ -127,34 +143,51 @@ def tile_qdense_kernel(
             )
 
         x_words_of = {0: load_x(0, ((0,), (1,)))}
+        load_scales(0)
+        load_words(0, 0)
+        x_words_of[0].update(load_x(0, ((2, 3),)))
+        load_scales(1)
+        load_words(1, 0)
         for w in range(PARTS):
             nc.sync.dma_start(
-                out=bias_rows[QUADRANT * w : QUADRANT * w + 1, :],
-                in_=bias_in[w].rearrange("(o n) -> o n", o=1),
+                out=bias_pieces[QUADRANT * w : QUADRANT * (w + 1), :],
+                in_=bias_in[w].rearrange("(b i) -> b i", i=QUADRANT),
             )
-        x_words_of[0].update(load_x(0, ((2, 3),)))
-        for w in range(PARTS):
+        for w in range(2, PARTS):
             load_words(w, 0)
             load_scales(w)
         for w in range(PARTS):
             load_words(w, 1)
         x_words_of[1] = load_x(1, ((0, 1), (2, 3)))
 
-        def bias_matmuls(half):
-            cols = slice(N_TILE * half, N_TILE * (half + 1))
-            filled = []
-            for o in range(PARTS):
-                number, bank = take_bank()
-                nc.tensor.matmul(out=bank[:], lhsT=signs[:, o, :], rhs=bias_rows[:, cols], start=True, stop=True)
-                filled.append((number, bank))
-            return filled
+        def bias_matmul():
+            number, bank = take_bank()
+            out = bank[:, 0 : PARTS * PIECES]
+            nc.tensor.matmul(
+                out=out,
+                lhsT=bias_lhs[:].rearrange("p q i -> p (q i)"),
+                rhs=select[:].rearrange("p o c -> p (o c)"),
+                start=True,
+                stop=True,
+            )
+            nc.scalar.copy(out=bias_cols[:].rearrange("p o b -> p (o b)"), in_=out)
+            free_banks.append(number)
 
-        def bias_copies(half, filled, chunks):
-            cols = slice(N_TILE * half, N_TILE * (half + 1))
-            for o in chunks:
-                number, bank = filled[o]
-                nc.scalar.copy(out=bias_all[:, o, cols], in_=bank[:])
-                free_banks.append(number)
+        def bias_widen(half):
+            pieces = slice(PIECES // COL_HALVES * half, PIECES // COL_HALVES * (half + 1))
+            for o in range(PARTS):
+                nc.scalar.copy(
+                    out=bias_wide[:, o, pieces, :],
+                    in_=bias_cols[:, o, pieces].unsqueeze(2).to_broadcast([P, PIECES // COL_HALVES, QUADRANT]),
+                )
+
+        def bias_turn(half):
+            pieces = slice(PIECES // COL_HALVES * half, PIECES // COL_HALVES * (half + 1))
+            for o in range(PARTS):
+                nc.vector.transpose(
+                    out=bias_all[:, o, N_TILE * half : N_TILE * (half + 1)],
+                    in_=bias_wide[:, o, pieces, :].rearrange("p b j -> p (b j)"),
+                )
 
         x_sorted_of = {}
 
@@ -193,31 +226,57 @@ def tile_qdense_kernel(
                 free_banks.append(number)
             return grouped
 
-        def quantise_pair(m, h, grouped):
-            chunks = slice(X_LOAD_CHUNKS * h, X_LOAD_CHUNKS * (h + 1))
+        def quantise(m, first, grouped):
+            chunks = slice(first, first + grouped.shape[1])
             nc.vector.quantize_mx(
                 out=x_codes[:, m, chunks].rearrange("p c g r -> p (c g r)").bitcast(FP8X4),
                 scales=x_planes[:, m, chunks].rearrange("p c g r -> p (c g r)"),
-                in_=grouped[:].rearrange("p c g r t -> p (c g r t)"),
+                in_=grouped.rearrange("p c g r t -> p (c g r t)"),
             )
 
-        def quantise_x(m):
+        def prepare_pair(h):
+            grouped = transpose_pair(0, h)
+            for j in range(X_LOAD_CHUNKS):
+                quantise(0, X_LOAD_CHUNKS * h + j, grouped[:, j : j + 1])
+
+        def prepare_block(m):
             pairs = range(PARTS // X_LOAD_CHUNKS)
             grouped_tiles = [transpose_pair(m, h) for h in pairs]
             for h in pairs:
-                quantise_pair(m, h, grouped_tiles[h])
+                quantise(m, X_LOAD_CHUNKS * h, grouped_tiles[h][:])
 
-        def multiply(m, half, order, together=1, next_x_before=None, first=0, width=N_TILE):
+        def multiply(m, half, steps, before=None, adds_from=0, first=0, width=N_TILE):
             inner = slice(first, first + width)
             cols = slice(N_TILE * half + first, N_TILE * half + first + width)
             groups = {}
             taken = {}
             partial = {}
-            for position in range(0, len(order), together):
-                if position == next_x_before:
-                    quantise_x(m + 1)
+            closed = []
+
+            def empty_closed():
+                for o, sign, number, bank in closed:
+                    op = ALU.add if sign > 0 else ALU.subtract
+                    if o not in partial:
+                        part = stage.tile([P, width], F32, tag="part")
+                        nc.vector.tensor_tensor(out=part[:], in0=bias_all[:, o, cols], in1=bank[:, 0:width], op=op)
+                        partial[o] = part
+                    else:
+                        result = stage.tile([P, width], F32, tag="result")
+                        nc.vector.tensor_tensor(out=result[:], in0=partial[o][:], in1=bank[:, 0:width], op=op)
+                        nc.sync.dma_start(
+                            out=out[P * m : P * (m + 1), CHUNK * o + cols.start : CHUNK * o + cols.stop],
+                            in_=result[:],
+                        )
+                    free_banks.append(number)
+                closed.clear()
+
+            for i, products in enumerate(steps):
+                if before is not None and i in before:
+                    before[i]()
+                if i >= adds_from:
+                    empty_closed()
                 step = []
-                for o, w in order[position : position + together]:
+                for o, w in products:
                     sign = SIGN[o][w]
                     members = len([v for v in range(PARTS) if SIGN[o][v] == sign])
                     if (o, sign) not in groups:
@@ -239,43 +298,34 @@ def tile_qdense_kernel(
                             start=(opens and g == 0),
                             stop=(closes and g == PASSES - 1),
                         )
-                for o, w, sign, number, bank, opens, closes in step:
-                    if not closes:
-                        continue
-                    op = ALU.add if sign > 0 else ALU.subtract
-                    if o not in partial:
-                        part = stage.tile([P, width], F32, tag="part")
-                        nc.vector.tensor_tensor(out=part[:], in0=bias_all[:, o, cols], in1=bank[:, 0:width], op=op)
-                        partial[o] = part
-                    else:
-                        result = stage.tile([P, width], F32, tag="result")
-                        nc.vector.tensor_tensor(out=result[:], in0=partial[o][:], in1=bank[:, 0:width], op=op)
-                        nc.sync.dma_start(
-                            out=out[P * m : P * (m + 1), CHUNK * o + cols.start : CHUNK * o + cols.stop],
-                            in_=result[:],
-                        )
-                    free_banks.append(number)
+                closed.extend([(o, sign, number, bank) for o, w, sign, number, bank, opens, closes in step if closes])
+                if i >= adds_from:
+                    empty_closed()
 
         def chunk_by_chunk(chunks):
-            return [(o, w) for o in chunks for w in weights_of(o)]
+            return [((o, w),) for o in chunks for w in weights_of(o)]
 
         for i in range(WARM_UP):
             number, bank = take_bank()
             nc.tensor.matmul(out=bank[:], lhsT=warm[:, 0:P], rhs=warm[:], start=True, stop=True)
             free_banks.append(number)
-        grouped = transpose_pair(0, 0)
-        filled = bias_matmuls(0)
-        bias_copies(0, filled, (0, 1))
-        quantise_pair(0, 0, grouped)
-        grouped = transpose_pair(0, 1)
-        bias_copies(0, filled, (2, 3))
-        quantise_pair(0, 1, grouped)
-        bias_copies(1, bias_matmuls(1), range(PARTS))
-        multiply(0, 0, WEIGHT_BY_WEIGHT, together=2)
+        nc.gpsimd.tensor_copy(out=bias_lhs[:], in_=bias_pieces[:].unsqueeze(1).to_broadcast([P, QUADRANTS, QUADRANT]))
+        prepare_pair(0)
+
+        def prepare_bias():
+            bias_matmul()
+            bias_widen(0)
+            bias_turn(0)
+            bias_widen(1)
+
+        multiply(
+            0, 0, FIRST_ROUND, before={2: lambda: prepare_pair(1), len(HEAD) + 1: prepare_bias}, adds_from=len(HEAD) + 1
+        )
         sort_x(1)
-        multiply(0, 1, PAIR_BY_PAIR, together=2, next_x_before=len(PAIR_BY_PAIR) - PARTS)
-        multiply(1, 0, PAIR_BY_PAIR, together=2)
-        multiply(1, 1, PAIR_BY_PAIR[: len(PAIR_BY_PAIR) // 2], together=2)
+        bias_turn(1)
+        multiply(0, 1, PAIR_BY_PAIR, before={len(PAIR_BY_PAIR) - 2: lambda: prepare_block(1)})
+        multiply(1, 0, PAIR_BY_PAIR)
+        multiply(1, 1, PAIR_BY_PAIR[: len(PAIR_BY_PAIR) // 2])
         multiply(1, 1, chunk_by_chunk((PARTS - 2,)))
         first = 0
         for width in LAST_WIDTHS:

@@ -35,10 +35,7 @@ FLOPS = 2 * ROWS * PARTS * CHUNK * PARTS * CHUNK
 X_CHUNK = ((0, 1, 2, 3), (1, 0, 3, 2), (2, 3, 0, 1), (3, 2, 1, 0))
 SIGN = ((1, -1, -1, -1), (1, 1, -1, 1), (1, 1, 1, -1), (1, -1, 1, 1))
 
-HEAD = (((0, 0),), ((1, 0),), ((0, 1), (1, 1)))
-FIRST_ROUND = HEAD + (((2, 0), (3, 0)), ((2, 1), (3, 1))) + tuple(
-    ((o, w), (o + 1, w)) for w in range(2, PARTS) for o in range(0, PARTS, 2)
-)
+WEIGHT_BY_WEIGHT = tuple(((o, w), (o + 1, w)) for w in range(PARTS) for o in range(0, PARTS, 2))
 PAIR_BY_PAIR = tuple(tuple((o, w) for o in pair) for pair in ((0, 1), (2, 3)) for w in range(PARTS))
 
 
@@ -143,9 +140,9 @@ def tile_qdense_kernel(
             )
 
         x_words_of = {0: load_x(0, ((0,), (1,)))}
+        x_words_of[0].update(load_x(0, ((2, 3),)))
         load_scales(0)
         load_words(0, 0)
-        x_words_of[0].update(load_x(0, ((2, 3),)))
         load_scales(1)
         load_words(1, 0)
         for w in range(PARTS):
@@ -245,12 +242,13 @@ def tile_qdense_kernel(
             for h in pairs:
                 quantise(m, X_LOAD_CHUNKS * h, grouped_tiles[h][:])
 
-        def multiply(m, half, steps, before=None, adds_from=0, first=0, width=N_TILE):
+        def multiply(m, half, steps, before=None, adds_from=0, shared=False, first=0, width=N_TILE):
             inner = slice(first, first + width)
             cols = slice(N_TILE * half + first, N_TILE * half + first + width)
             groups = {}
             taken = {}
             partial = {}
+            emptied = {}
             closed = []
 
             def empty_closed():
@@ -258,7 +256,11 @@ def tile_qdense_kernel(
                     op = ALU.add if sign > 0 else ALU.subtract
                     if o not in partial:
                         part = stage.tile([P, width], F32, tag="part")
-                        nc.vector.tensor_tensor(out=part[:], in0=bias_all[:, o, cols], in1=bank[:, 0:width], op=op)
+                        if shared:
+                            nc.gpsimd.tensor_tensor(out=part[:], in0=bias_all[:, o, cols], in1=emptied[o][:], op=op)
+                        else:
+                            nc.vector.tensor_tensor(out=part[:], in0=bias_all[:, o, cols], in1=bank[:, 0:width], op=op)
+                            free_banks.append(number)
                         partial[o] = part
                     else:
                         result = stage.tile([P, width], F32, tag="result")
@@ -267,7 +269,7 @@ def tile_qdense_kernel(
                             out=out[P * m : P * (m + 1), CHUNK * o + cols.start : CHUNK * o + cols.stop],
                             in_=result[:],
                         )
-                    free_banks.append(number)
+                        free_banks.append(number)
                 closed.clear()
 
             for i, products in enumerate(steps):
@@ -298,7 +300,15 @@ def tile_qdense_kernel(
                             start=(opens and g == 0),
                             stop=(closes and g == PASSES - 1),
                         )
-                closed.extend([(o, sign, number, bank) for o, w, sign, number, bank, opens, closes in step if closes])
+                for o, w, sign, number, bank, opens, closes in step:
+                    if not closes:
+                        continue
+                    closed.append((o, sign, number, bank))
+                    if shared and o not in emptied:
+                        copied = stage.tile([P, N_TILE], F32, tag="emptied")
+                        nc.scalar.copy(out=copied[:], in_=bank[:])
+                        free_banks.append(number)
+                        emptied[o] = copied
                 if i >= adds_from:
                     empty_closed()
 
@@ -311,19 +321,30 @@ def tile_qdense_kernel(
             free_banks.append(number)
         nc.gpsimd.tensor_copy(out=bias_lhs[:], in_=bias_pieces[:].unsqueeze(1).to_broadcast([P, QUADRANTS, QUADRANT]))
         prepare_pair(0)
+        prepare_pair(1)
 
         def prepare_bias():
             bias_matmul()
             bias_widen(0)
             bias_turn(0)
-            bias_widen(1)
 
         multiply(
-            0, 0, FIRST_ROUND, before={2: lambda: prepare_pair(1), len(HEAD) + 1: prepare_bias}, adds_from=len(HEAD) + 1
+            0,
+            0,
+            WEIGHT_BY_WEIGHT,
+            before={3: prepare_bias, 5: lambda: bias_widen(1)},
+            adds_from=3,
+            shared=True,
         )
         sort_x(1)
         bias_turn(1)
-        multiply(0, 1, PAIR_BY_PAIR, before={len(PAIR_BY_PAIR) - 2: lambda: prepare_block(1)})
+        multiply(
+            0,
+            1,
+            WEIGHT_BY_WEIGHT,
+            before={len(WEIGHT_BY_WEIGHT) - 2: lambda: prepare_block(1)},
+            shared=True,
+        )
         multiply(1, 0, PAIR_BY_PAIR)
         multiply(1, 1, PAIR_BY_PAIR[: len(PAIR_BY_PAIR) // 2])
         multiply(1, 1, chunk_by_chunk((PARTS - 2,)))

@@ -28,6 +28,7 @@ PIECES = CHUNK // QUADRANT
 SCALE_ROWS = 4
 X_LOAD_CHUNKS = 2
 WARM_UP = 5
+FILLERS = 2
 LAST_WIDTHS = (256, 256)
 
 FLOPS = 2 * ROWS * PARTS * CHUNK * PARTS * CHUNK
@@ -315,13 +316,18 @@ def tile_qdense_kernel(
         def chunk_by_chunk(chunks):
             return [((o, w),) for o in chunks for w in weights_of(o)]
 
-        for i in range(WARM_UP):
-            number, bank = take_bank()
-            nc.tensor.matmul(out=bank[:], lhsT=warm[:, 0:P], rhs=warm[:], start=True, stop=True)
-            free_banks.append(number)
+        def keep_warm(count):
+            for i in range(count):
+                number, bank = take_bank()
+                nc.tensor.matmul(out=bank[:], lhsT=warm[:, 0:P], rhs=warm[:], start=True, stop=True)
+                free_banks.append(number)
+
+        keep_warm(WARM_UP)
         nc.gpsimd.tensor_copy(out=bias_lhs[:], in_=bias_pieces[:].unsqueeze(1).to_broadcast([P, QUADRANTS, QUADRANT]))
         prepare_pair(0)
+        keep_warm(FILLERS)
         prepare_pair(1)
+        keep_warm(FILLERS)
 
         def prepare_bias():
             bias_matmul()

@@ -71,6 +71,7 @@ def tile_qdense_kernel(
         keep = ctx.enter_context(tc.tile_pool(name="keep", bufs=1))
         x_pool = ctx.enter_context(tc.tile_pool(name="x_pool", bufs=ROW_BLOCKS * PARTS))
         stage = ctx.enter_context(tc.tile_pool(name="stage", bufs=4))
+        totals = ctx.enter_context(tc.tile_pool(name="totals", bufs=COL_HALVES * PARTS))
         psum = ctx.enter_context(tc.psum_pool(name="psum", bufs=1))
 
         free_banks = list(range(PSUM_BANKS))
@@ -82,7 +83,7 @@ def tile_qdense_kernel(
             return number, bank
 
         w_words = keep.tile([P, PARTS, COL_HALVES, PASSES, N_TILE], U32, align_bytes=64)
-        w_planes = keep.tile([P, PARTS, CHUNK], U8, align_bytes=64)
+        w_planes = keep.tile([P, PARTS, COL_HALVES, N_TILE], U8, align_bytes=64)
         x_codes = keep.tile([P, ROW_BLOCKS, PARTS, PASSES, P], U32, align_bytes=64)
         x_planes = keep.tile([P, ROW_BLOCKS, PARTS, PASSES, P], U8, align_bytes=64)
         ident = keep.tile([P, P], F32)
@@ -125,12 +126,15 @@ def tile_qdense_kernel(
                     words[c] = x_raw[:, CHUNK * i : CHUNK * (i + 1)].bitcast(F32)
             return words
 
-        def load_scales(w):
+        def load_scales(w, halves):
+            cols = slice(N_TILE * halves[0], N_TILE * (halves[-1] + 1))
             for quad in range(QUADRANTS):
                 first = QUADRANT * quad
                 nc.sync.dma_start(
-                    out=w_planes[first : first + PASSES * SCALE_ROWS, w, :].bitcast(I32),
-                    in_=scales_in[w][:, SCALE_ROWS * quad : SCALE_ROWS * (quad + 1), :].bitcast(I32),
+                    out=w_planes[first : first + PASSES * SCALE_ROWS, w, halves[0] : halves[-1] + 1, :]
+                    .rearrange("p h n -> p (h n)")
+                    .bitcast(I32),
+                    in_=scales_in[w][:, SCALE_ROWS * quad : SCALE_ROWS * (quad + 1), cols].bitcast(I32),
                 )
 
         def load_words(w, half):
@@ -140,23 +144,34 @@ def tile_qdense_kernel(
                 in_=words_in[w].rearrange("g p n t -> p g (n t)")[:, :, byte_cols].bitcast(I32),
             )
 
+        def load_words_of_pass(w, half, g):
+            byte_cols = slice(PACK * N_TILE * half, PACK * N_TILE * (half + 1))
+            nc.sync.dma_start(
+                out=w_words[:, w, half, g, :].bitcast(I32),
+                in_=words_in[w][g].rearrange("p n t -> p (n t)")[:, byte_cols].bitcast(I32),
+            )
+
         x_words_of = {0: load_x(0, ((0,), (1,)))}
         x_words_of[0].update(load_x(0, ((2, 3),)))
-        load_scales(0)
-        load_words(0, 0)
-        load_scales(1)
+        load_scales(0, (0,))
+        for g in range(PASSES):
+            load_words_of_pass(0, 0, g)
+        load_scales(1, (0,))
         load_words(1, 0)
+        for w in range(2, PARTS):
+            load_scales(w, (0, 1))
+            load_words(w, 0)
         for w in range(PARTS):
             nc.sync.dma_start(
                 out=bias_pieces[QUADRANT * w : QUADRANT * (w + 1), :],
                 in_=bias_in[w].rearrange("(b i) -> b i", i=QUADRANT),
             )
-        for w in range(2, PARTS):
-            load_words(w, 0)
-            load_scales(w)
         for w in range(PARTS):
+            if w == PARTS - 1:
+                x_words_of[1] = load_x(1, ((0, 1), (2, 3)))
             load_words(w, 1)
-        x_words_of[1] = load_x(1, ((0, 1), (2, 3)))
+            if w < 2:
+                load_scales(w, (1,))
 
         def bias_matmul():
             number, bank = take_bank()
@@ -243,41 +258,20 @@ def tile_qdense_kernel(
             for h in pairs:
                 quantise(m, X_LOAD_CHUNKS * h, grouped_tiles[h][:])
 
-        def multiply(m, half, steps, before=None, adds_from=0, shared=False, first=0, width=N_TILE):
+        def store(m, o, cols, result):
+            nc.sync.dma_start(
+                out=out[P * m : P * (m + 1), CHUNK * o + cols.start : CHUNK * o + cols.stop], in_=result[:]
+            )
+
+        def multiply(m, half, steps, before=None, without_bias=None, first=0, width=N_TILE):
             inner = slice(first, first + width)
             cols = slice(N_TILE * half + first, N_TILE * half + first + width)
             groups = {}
             taken = {}
             partial = {}
-            emptied = {}
-            closed = []
-
-            def empty_closed():
-                for o, sign, number, bank in closed:
-                    op = ALU.add if sign > 0 else ALU.subtract
-                    if o not in partial:
-                        part = stage.tile([P, width], F32, tag="part")
-                        if shared:
-                            nc.gpsimd.tensor_tensor(out=part[:], in0=bias_all[:, o, cols], in1=emptied[o][:], op=op)
-                        else:
-                            nc.vector.tensor_tensor(out=part[:], in0=bias_all[:, o, cols], in1=bank[:, 0:width], op=op)
-                            free_banks.append(number)
-                        partial[o] = part
-                    else:
-                        result = stage.tile([P, width], F32, tag="result")
-                        nc.vector.tensor_tensor(out=result[:], in0=partial[o][:], in1=bank[:, 0:width], op=op)
-                        nc.sync.dma_start(
-                            out=out[P * m : P * (m + 1), CHUNK * o + cols.start : CHUNK * o + cols.stop],
-                            in_=result[:],
-                        )
-                        free_banks.append(number)
-                closed.clear()
-
             for i, products in enumerate(steps):
                 if before is not None and i in before:
                     before[i]()
-                if i >= adds_from:
-                    empty_closed()
                 step = []
                 for o, w in products:
                     sign = SIGN[o][w]
@@ -297,21 +291,40 @@ def tile_qdense_kernel(
                             lhsT=x_codes[:, m, X_CHUNK[o][w], g, :].bitcast(FP8X4),
                             lhsT_scale=x_planes[:, m, X_CHUNK[o][w], g, :],
                             rhs=w_words[:, w, half, g, inner].bitcast(FP8X4),
-                            rhs_scale=w_planes[SCALE_ROWS * g : P, w, cols],
+                            rhs_scale=w_planes[SCALE_ROWS * g : P, w, half, inner],
                             start=(opens and g == 0),
                             stop=(closes and g == PASSES - 1),
                         )
                 for o, w, sign, number, bank, opens, closes in step:
                     if not closes:
                         continue
-                    closed.append((o, sign, number, bank))
-                    if shared and o not in emptied:
-                        copied = stage.tile([P, N_TILE], F32, tag="emptied")
-                        nc.scalar.copy(out=copied[:], in_=bank[:])
-                        free_banks.append(number)
-                        emptied[o] = copied
-                if i >= adds_from:
-                    empty_closed()
+                    op = ALU.add if sign > 0 else ALU.subtract
+                    if without_bias is not None and o not in partial:
+                        part = stage.tile([P, width], F32, tag="part")
+                        nc.scalar.copy(out=part[:], in_=bank[:, 0:width])
+                        partial[o] = part
+                    elif without_bias is not None:
+                        plus, minus = (bank, partial[o]) if sign > 0 else (partial[o], bank)
+                        total = totals.tile([P, width], F32, tag="total")
+                        nc.vector.tensor_tensor(
+                            out=total[:], in0=plus[:, 0:width], in1=minus[:, 0:width], op=ALU.subtract
+                        )
+                        without_bias.append((m, o, cols, total))
+                    elif o not in partial:
+                        part = stage.tile([P, width], F32, tag="part")
+                        nc.vector.tensor_tensor(out=part[:], in0=bias_all[:, o, cols], in1=bank[:, 0:width], op=op)
+                        partial[o] = part
+                    else:
+                        result = stage.tile([P, width], F32, tag="result")
+                        nc.vector.tensor_tensor(out=result[:], in0=partial[o][:], in1=bank[:, 0:width], op=op)
+                        store(m, o, cols, result)
+                    free_banks.append(number)
+
+        def add_bias(without_bias):
+            for m, o, cols, total in without_bias:
+                with_bias = stage.tile([P, N_TILE], F32, tag="with_bias")
+                nc.gpsimd.tensor_tensor(out=with_bias[:], in0=bias_all[:, o, cols], in1=total[:], op=ALU.add)
+                store(m, o, cols, with_bias)
 
         def chunk_by_chunk(chunks):
             return [((o, w),) for o in chunks for w in weights_of(o)]
@@ -327,30 +340,25 @@ def tile_qdense_kernel(
         prepare_pair(0)
         keep_warm(FILLERS)
         prepare_pair(1)
-        keep_warm(FILLERS)
+        keep_warm(FILLERS // 2)
 
-        def prepare_bias():
-            bias_matmul()
-            bias_widen(0)
-            bias_turn(0)
-
-        multiply(
-            0,
-            0,
-            WEIGHT_BY_WEIGHT,
-            before={3: prepare_bias, 5: lambda: bias_widen(1)},
-            adds_from=3,
-            shared=True,
-        )
+        without_bias = []
+        multiply(0, 0, WEIGHT_BY_WEIGHT, before={len(WEIGHT_BY_WEIGHT) - 1: bias_matmul}, without_bias=without_bias)
+        bias_widen(0)
+        bias_turn(0)
+        add_bias(without_bias)
         sort_x(1)
-        bias_turn(1)
+        without_bias = []
         multiply(
             0,
             1,
             WEIGHT_BY_WEIGHT,
             before={len(WEIGHT_BY_WEIGHT) - 2: lambda: prepare_block(1)},
-            shared=True,
+            without_bias=without_bias,
         )
+        bias_widen(1)
+        bias_turn(1)
+        add_bias(without_bias)
         multiply(1, 0, PAIR_BY_PAIR)
         multiply(1, 1, PAIR_BY_PAIR[: len(PAIR_BY_PAIR) // 2])
         multiply(1, 1, chunk_by_chunk((PARTS - 2,)))

from contextlib import ExitStack

import concourse.mybir as mybir
from concourse.masks import make_identity

F32 = mybir.dt.float32
BF16 = mybir.dt.bfloat16
I32 = mybir.dt.int32
U32 = mybir.dt.uint32
U8 = mybir.dt.uint8
FP8X4 = mybir.dt.float8_e4m3fn_x4
ALU = mybir.AluOpType

P = 128
PACK = 4
K_PASS = P * PACK
ROWS = 256
CHUNK = 1024
PARTS = 4
PASSES = CHUNK // K_PASS
ROW_BLOCKS = ROWS // P
N_TILE = 512
COL_HALVES = CHUNK // N_TILE
PSUM_BANKS = 8
QUADRANT = 32
QUADRANTS = P // QUADRANT
PIECES = CHUNK // QUADRANT
SCALE_ROWS = 4
X_LOAD_CHUNKS = 2
WARM_UP = 5
FILLERS = 2
LAST_WIDTHS = (256, 256)

FLOPS = 2 * ROWS * PARTS * CHUNK * PARTS * CHUNK

X_CHUNK = ((0, 1, 2, 3), (1, 0, 3, 2), (2, 3, 0, 1), (3, 2, 1, 0))
SIGN = ((1, -1, -1, -1), (1, 1, -1, 1), (1, 1, 1, -1), (1, -1, 1, 1))

WEIGHT_BY_WEIGHT = tuple(((o, w), (o + 1, w)) for w in range(PARTS) for o in range(0, PARTS, 2))
PAIR_BY_PAIR = tuple(tuple((o, w) for o in pair) for pair in ((0, 1), (2, 3)) for w in range(PARTS))


def weights_of(o):
    return sorted(range(PARTS), key=lambda w: len([v for v in range(PARTS) if SIGN[o][v] == SIGN[o][w]]))


def tile_qdense_kernel(
    tc,
    x,
    W_rr_words,
    W_rr_scales,
    W_ri_words,
    W_ri_scales,
    W_rj_words,
    W_rj_scales,
    W_rk_words,
    W_rk_scales,
    b_rr,
    b_ri,
    b_rj,
    b_rk,
    out,
):
    nc = tc.nc
    words_in = (W_rr_words, W_ri_words, W_rj_words, W_rk_words)
    scales_in = (W_rr_scales, W_ri_scales, W_rj_scales, W_rk_scales)
    bias_in = (b_rr, b_ri, b_rj, b_rk)

    with ExitStack() as ctx:
        ctx.enter_context(tc.manual_schedule())
        keep = ctx.enter_context(tc.tile_pool(name="keep", bufs=1))
        x_pool = ctx.enter_context(tc.tile_pool(name="x_pool", bufs=ROW_BLOCKS * PARTS))
        stage = ctx.enter_context(tc.tile_pool(name="stage", bufs=4))
        totals = ctx.enter_context(tc.tile_pool(name="totals", bufs=COL_HALVES * PARTS))
        psum = ctx.enter_context(tc.psum_pool(name="psum", bufs=1))

        free_banks = list(range(PSUM_BANKS))

        def take_bank():
            number = free_banks[0]
            free_banks.remove(number)
            bank = psum.tile([P, N_TILE], F32, tag="bank%d" % number)
            return number, bank

        w_words = keep.tile([P, PARTS, COL_HALVES, PASSES, N_TILE], U32, align_bytes=64)
        w_planes = keep.tile([P, PARTS, COL_HALVES, N_TILE], U8, align_bytes=64)
        x_codes = keep.tile([P, ROW_BLOCKS, PARTS, PASSES, P], U32, align_bytes=64)
        x_planes = keep.tile([P, ROW_BLOCKS, PARTS, PASSES, P], U8, align_bytes=64)
        ident = keep.tile([P, P], F32)
        bias_pieces = keep.tile([P, QUADRANT], BF16)
        bias_lhs = keep.tile([P, QUADRANTS, QUADRANT], BF16)
        signs = keep.tile([P, PARTS], F32)
        select = keep.tile([P, PARTS, QUADRANT], BF16)
        bias_cols = keep.tile([P, PARTS, PIECES], F32)
        bias_wide = keep.tile([P, PARTS, PIECES, QUADRANT], F32, align_bytes=64)
        bias_all = keep.tile([P, PARTS, CHUNK], F32, align_bytes=64)

        warm = keep.tile([P, N_TILE], BF16)
        nc.gpsimd.memset(warm[:].bitcast(F32), 0.0)
        for w in range(PARTS):
            nc.vector.memset(w_planes[:, w].bitcast(I32), 0)
        make_identity(nc, ident[:])
        nc.gpsimd.memset(signs[:], 1.0)
        for o in range(PARTS):
            for w in range(PARTS):
                if SIGN[o][w] < 0:
                    nc.gpsimd.memset(signs[QUADRANT * w : QUADRANT * (w + 1), o : o + 1], -1.0)
        for w in range(PARTS):
            rows = slice(QUADRANT * w, QUADRANT * (w + 1))
            shape = [QUADRANT, PARTS, QUADRANT]
            nc.gpsimd.tensor_tensor(
                out=select[rows],
                in0=ident[rows, rows].unsqueeze(1).to_broadcast(shape),
                in1=signs[rows].unsqueeze(2).to_broadcast(shape),
                op=ALU.mult,
            )

        def load_x(m, loads):
            words = {}
            for chunks in loads:
                x_raw = x_pool.tile([P, CHUNK * len(chunks)], BF16, tag="x_raw")
                nc.sync.dma_start(
                    out=x_raw[:], in_=x[P * m : P * (m + 1), CHUNK * chunks[0] : CHUNK * (chunks[-1] + 1)]
                )
                for i, c in enumerate(chunks):
                    words[c] = x_raw[:, CHUNK * i : CHUNK * (i + 1)].bitcast(F32)
            return words

        def load_scales(w, halves):
            cols = slice(N_TILE * halves[0], N_TILE * (halves[-1] + 1))
            for quad in range(QUADRANTS):
                first = QUADRANT * quad
                nc.sync.dma_start(
                    out=w_planes[first : first + PASSES * SCALE_ROWS, w, halves[0] : halves[-1] + 1, :]
                    .rearrange("p h n -> p (h n)")
                    .bitcast(I32),
                    in_=scales_in[w][:, SCALE_ROWS * quad : SCALE_ROWS * (quad + 1), cols].bitcast(I32),
                )

        def load_words(w, half):
            byte_cols = slice(PACK * N_TILE * half, PACK * N_TILE * (half + 1))
            nc.sync.dma_start(
                out=w_words[:, w, half, :, :].bitcast(I32),
                in_=words_in[w].rearrange("g p n t -> p g (n t)")[:, :, byte_cols].bitcast(I32),
            )

        def load_words_of_pass(w, half, g):
            byte_cols = slice(PACK * N_TILE * half, PACK * N_TILE * (half + 1))
            nc.sync.dma_start(
                out=w_words[:, w, half, g, :].bitcast(I32),
                in_=words_in[w][g].rearrange("p n t -> p (n t)")[:, byte_cols].bitcast(I32),
            )

        x_words_of = {0: load_x(0, ((0,), (1,)))}
        x_words_of[0].update(load_x(0, ((2, 3),)))
        load_scales(0, (0,))
        for g in range(PASSES):
            load_words_of_pass(0, 0, g)
        load_scales(1, (0,))
        load_words(1, 0)
        for w in range(2, PARTS):
            load_scales(w, (0, 1))
            load_words(w, 0)
        for w in range(PARTS):
            nc.sync.dma_start(
                out=bias_pieces[QUADRANT * w : QUADRANT * (w + 1), :],
                in_=bias_in[w].rearrange("(b i) -> b i", i=QUADRANT),
            )
        for w in range(PARTS):
            if w == PARTS - 1:
                x_words_of[1] = load_x(1, ((0, 1), (2, 3)))
            load_words(w, 1)
            if w < 2:
                load_scales(w, (1,))

        def bias_matmul():
            number, bank = take_bank()
            out = bank[:, 0 : PARTS * PIECES]
            nc.tensor.matmul(
                out=out,
                lhsT=bias_lhs[:].rearrange("p q i -> p (q i)"),
                rhs=select[:].rearrange("p o c -> p (o c)"),
                start=True,
                stop=True,
            )
            nc.scalar.copy(out=bias_cols[:].rearrange("p o b -> p (o b)"), in_=out)
            free_banks.append(number)

        def bias_widen(half):
            pieces = slice(PIECES // COL_HALVES * half, PIECES // COL_HALVES * (half + 1))
            for o in range(PARTS):
                nc.scalar.copy(
                    out=bias_wide[:, o, pieces, :],
                    in_=bias_cols[:, o, pieces].unsqueeze(2).to_broadcast([P, PIECES // COL_HALVES, QUADRANT]),
                )

        def bias_turn(half):
            pieces = slice(PIECES // COL_HALVES * half, PIECES // COL_HALVES * (half + 1))
            for o in range(PARTS):
                nc.vector.transpose(
                    out=bias_all[:, o, N_TILE * half : N_TILE * (half + 1)],
                    in_=bias_wide[:, o, pieces, :].rearrange("p b j -> p (b j)"),
                )

        x_sorted_of = {}

        def sort_x(m):
            x_sorted_of[m] = []
            for c in range(PARTS):
                x_sorted = x_pool.tile([P, PASSES, 2, P], F32, tag="x_sorted")
                nc.scalar.copy(
                    out=x_sorted[:],
                    in_=x_words_of[m][c].rearrange("p (g i u) -> p g u i", g=PASSES, u=2),
                )
                x_sorted_of[m].append(x_sorted)

        def transpose_pair(m, h):
            grouped = stage.tile([P, X_LOAD_CHUNKS, PASSES, P, PACK], BF16, tag="grouped", align_bytes=64)
            for j in range(X_LOAD_CHUNKS):
                c = X_LOAD_CHUNKS * h + j
                number, bank = take_bank()
                for g in range(PASSES):
                    first = (K_PASS // 2) * g
                    for u in range(2):
                        if m in x_sorted_of:
                            words = x_sorted_of[m][c][:, g, u, :]
                        else:
                            words = x_words_of[m][c][:, first + u : first + K_PASS // 2 : 2]
                        nc.tensor.transpose(
                            bank[:].rearrange("p (g u r) -> p g u r", g=PASSES, u=2)[:, g, u, :],
                            words,
                            ident[:],
                        )
                copy = nc.vector.tensor_copy if j % 2 == 0 else nc.scalar.copy
                copy(
                    out=grouped[:, j].bitcast(F32),
                    in_=bank[:].rearrange("p (g u r) -> p g r u", g=PASSES, u=2),
                )
                free_banks.append(number)
            return grouped

        def quantise(m, first, grouped):
            chunks = slice(first, first + grouped.shape[1])
            nc.vector.quantize_mx(
                out=x_codes[:, m, chunks].rearrange("p c g r -> p (c g r)").bitcast(FP8X4),
                scales=x_planes[:, m, chunks].rearrange("p c g r -> p (c g r)"),
                in_=grouped.rearrange("p c g r t -> p (c g r t)"),
            )

        def prepare_pair(h):
            grouped = transpose_pair(0, h)
            for j in range(X_LOAD_CHUNKS):
                quantise(0, X_LOAD_CHUNKS * h + j, grouped[:, j : j + 1])

        def prepare_block(m):
            pairs = range(PARTS // X_LOAD_CHUNKS)
            grouped_tiles = [transpose_pair(m, h) for h in pairs]
            for h in pairs:
                quantise(m, X_LOAD_CHUNKS * h, grouped_tiles[h][:])

        def store(m, o, cols, result):
            nc.sync.dma_start(
                out=out[P * m : P * (m + 1), CHUNK * o + cols.start : CHUNK * o + cols.stop], in_=result[:]
            )

        def multiply(m, half, steps, before=None, without_bias=None, first=0, width=N_TILE):
            inner = slice(first, first + width)
            cols = slice(N_TILE * half + first, N_TILE * half + first + width)
            groups = {}
            taken = {}
            partial = {}
            for i, products in enumerate(steps):
                if before is not None and i in before:
                    before[i]()
                step = []
                for o, w in products:
                    sign = SIGN[o][w]
                    members = len([v for v in range(PARTS) if SIGN[o][v] == sign])
                    if (o, sign) not in groups:
                        groups[(o, sign)] = take_bank()
                        taken[(o, sign)] = 0
                    number, bank = groups[(o, sign)]
                    opens = taken[(o, sign)] == 0
                    taken[(o, sign)] = taken[(o, sign)] + 1
                    closes = taken[(o, sign)] == members
                    step.append((o, w, sign, number, bank, opens, closes))
                for g in range(PASSES):
                    for o, w, sign, number, bank, opens, closes in step:
                        nc.tensor.matmul_mx(
                            out=bank[:, 0:width],
                            lhsT=x_codes[:, m, X_CHUNK[o][w], g, :].bitcast(FP8X4),
                            lhsT_scale=x_planes[:, m, X_CHUNK[o][w], g, :],
                            rhs=w_words[:, w, half, g, inner].bitcast(FP8X4),
                            rhs_scale=w_planes[SCALE_ROWS * g : P, w, half, inner],
                            start=(opens and g == 0),
                            stop=(closes and g == PASSES - 1),
                        )
                for o, w, sign, number, bank, opens, closes in step:
                    if not closes:
                        continue
                    op = ALU.add if sign > 0 else ALU.subtract
                    if without_bias is not None and o not in partial:
                        part = stage.tile([P, width], F32, tag="part")
                        nc.scalar.copy(out=part[:], in_=bank[:, 0:width])
                        partial[o] = part
                    elif without_bias is not None:
                        plus, minus = (bank, partial[o]) if sign > 0 else (partial[o], bank)
                        total = totals.tile([P, width], F32, tag="total")
                        nc.vector.tensor_tensor(
                            out=total[:], in0=plus[:, 0:width], in1=minus[:, 0:width], op=ALU.subtract
                        )
                        without_bias.append((m, o, cols, total))
                    elif o not in partial:
                        part = stage.tile([P, width], F32, tag="part")
                        nc.vector.tensor_tensor(out=part[:], in0=bias_all[:, o, cols], in1=bank[:, 0:width], op=op)
                        partial[o] = part
                    else:
                        result = stage.tile([P, width], F32, tag="result")
                        nc.vector.tensor_tensor(out=result[:], in0=partial[o][:], in1=bank[:, 0:width], op=op)
                        store(m, o, cols, result)
                    free_banks.append(number)

        def add_bias(without_bias):
            for m, o, cols, total in without_bias:
                with_bias = stage.tile([P, N_TILE], F32, tag="with_bias")
                nc.gpsimd.tensor_tensor(out=with_bias[:], in0=bias_all[:, o, cols], in1=total[:], op=ALU.add)
                store(m, o, cols, with_bias)

        def chunk_by_chunk(chunks):
            return [((o, w),) for o in chunks for w in weights_of(o)]

        def keep_warm(count):
            for i in range(count):
                number, bank = take_bank()
                nc.tensor.matmul(out=bank[:], lhsT=warm[:, 0:P], rhs=warm[:], start=True, stop=True)
                free_banks.append(number)

        keep_warm(WARM_UP)
        nc.gpsimd.tensor_copy(out=bias_lhs[:], in_=bias_pieces[:].unsqueeze(1).to_broadcast([P, QUADRANTS, QUADRANT]))
        prepare_pair(0)
        keep_warm(FILLERS)
        prepare_pair(1)
        keep_warm(FILLERS // 2)

        without_bias = []
        multiply(0, 0, WEIGHT_BY_WEIGHT, before={len(WEIGHT_BY_WEIGHT) - 1: bias_matmul}, without_bias=without_bias)
        bias_widen(0)
        bias_turn(0)
        add_bias(without_bias)
        sort_x(1)
        without_bias = []
        multiply(
            0,
            1,
            WEIGHT_BY_WEIGHT,
            before={len(WEIGHT_BY_WEIGHT) - 2: lambda: prepare_block(1)},
            without_bias=without_bias,
        )
        bias_widen(1)
        bias_turn(1)
        add_bias(without_bias)
        multiply(1, 0, PAIR_BY_PAIR)
        multiply(1, 1, PAIR_BY_PAIR[: len(PAIR_BY_PAIR) // 2])
        multiply(1, 1, chunk_by_chunk((PARTS - 2,)))
        first = 0
        for width in LAST_WIDTHS:
            multiply(1, 1, chunk_by_chunk((PARTS - 1,)), first=first, width=width)
            first += width
